import numpy as np
import ml_dtypes


BF16 = ml_dtypes.bfloat16


def bf(x):
    return np.asarray(x, np.float32).astype(BF16)


def f64(x):
    return np.asarray(x).astype(np.float64)


E2M1 = np.array([0.0, 0.5, 1.0, 1.5, 2.0, 3.0, 4.0, 6.0, -0.0, -0.5, -1.0, -1.5, -2.0, -3.0, -4.0, -6.0])


def pack_weight(w, fmt):
    k, n = w.shape
    w = f64(bf(w)).reshape(k // 32, 32, n)
    amax = np.abs(w).max(1)
    if fmt == "e4m3":
        byte = np.frexp(amax)[1] - 1 + 127 - 7
    else:
        mant, ex = np.frexp(amax / 6.0)
        byte = np.where(mant > 0.5, ex, ex - 1) + 127
    byte = np.clip(np.where(amax > 0, byte, 1), 1, 254)
    scaled = (w * np.exp2(127.0 - byte)[:, None, :]).reshape(k, n).astype(np.float32)
    by_word = np.ascontiguousarray(scaled.reshape(k // 512, 128, 4, n).transpose(0, 1, 3, 2))
    if fmt == "e4m3":
        words = by_word.astype(ml_dtypes.float8_e4m3fn).view(np.uint8)
    else:
        c = by_word.astype(ml_dtypes.float4_e2m1fn).view(np.uint8) & 0xF
        words = c[..., 0::2] | (c[..., 1::2] << 4)
    return np.ascontiguousarray(words), np.ascontiguousarray(byte.astype(np.uint8).reshape(k // 512, 16, n))


def unpack_weight(words, scales, fmt):
    g, p, n, _ = words.shape
    if fmt == "e4m3":
        vals = np.ascontiguousarray(words).view(ml_dtypes.float8_e4m3fn).astype(np.float64)
    else:
        nib = np.empty((g, p, n, 4), np.uint8)
        nib[..., 0::2] = words & 0xF
        nib[..., 1::2] = words >> 4
        vals = E2M1[nib]
    vals = vals * np.repeat(np.exp2(scales.astype(np.float64) - 127.0), 8, axis=1)[..., None]
    return vals.transpose(0, 1, 3, 2).reshape(g * 512, n)

def pack4(w):
    words, scales = pack_weight(w, "e2m1")
    return words.reshape(words.shape[0], 128, -1), scales


def unpack4(words, scales):
    return unpack_weight(words.reshape(words.shape[0], 128, -1, 2), scales, "e2m1")


def kspread(k):
    return np.exp2(np.repeat(np.random.randint(-6, 7, k // 32), 32).astype(np.float64))


B, S, E, H, KV, D, W = 1, 2048, 4096, 8, 4, 256, 512
ROPE_BASE = 10000.0


def rope_tables():
    inv_freq = 1.0 / (ROPE_BASE ** (np.arange(0, D, 2) / D))
    ang = np.outer(np.arange(S), inv_freq)
    emb = np.concatenate([ang, ang], -1)
    return np.cos(emb), np.sin(emb)


def apply_rope(x, cos, sin):
    x1, x2 = np.split(x, 2, axis=-1)
    rot = np.concatenate([-x2, x1], axis=-1)
    return x * cos[None, :, None, :] + rot * sin[None, :, None, :]


def setup_inputs():
    s = kspread(E)
    hidden_states = np.random.standard_normal((B, S, E)) * s
    hidden_states_words, hidden_states_scales = pack4(np.ascontiguousarray(hidden_states.reshape(B * S, E).T))
    Wq_words, Wq_scales = pack4(np.random.standard_normal((E, H * D)) * 0.8 / np.sqrt(E) / s[:, None])
    Wk_words, Wk_scales = pack4(np.random.standard_normal((E, KV * D)) * 0.8 / np.sqrt(E) / s[:, None])
    return {"hidden_states_words": hidden_states_words, "hidden_states_scales": hidden_states_scales,
            "Wq_words": Wq_words, "Wq_scales": Wq_scales,
            "Wk_words": Wk_words, "Wk_scales": Wk_scales}


def reference(hidden_states_words, hidden_states_scales, Wq_words, Wq_scales, Wk_words, Wk_scales):
    xq = unpack4(hidden_states_words, hidden_states_scales).T.reshape(B, S, E)
    q = (xq @ unpack4(Wq_words, Wq_scales)).reshape(B, S, H, D)
    k = (xq @ unpack4(Wk_words, Wk_scales)).reshape(B, S, KV, D)
    cos, sin = rope_tables()
    return apply_rope(q, cos, sin), apply_rope(k, cos, sin)

@@ -1,0 +1,251 @@
+import math
+from contextlib import ExitStack
+
+import concourse.mybir as mybir
+
+F32 = mybir.dt.float32
+I32 = mybir.dt.int32
+U8 = mybir.dt.uint8
+FP4X4 = mybir.dt.float4_e2m1fn_x4
+ALU = mybir.AluOpType
+ACT = mybir.ActivationFunctionType
+
+TOKENS = 2048
+FEATURES = 4096
+Q_COLS = 2048
+K_COLS = 1024
+FLOPS = 2 * TOKENS * FEATURES * (Q_COLS + K_COLS)
+
+P = 128
+PASSES = FEATURES // 512
+TOKEN_TILES = TOKENS // P
+BLOCK = 512
+HALF = 128
+HEAD = 2 * HALF
+Q_BLOCKS = Q_COLS // BLOCK
+BLOCKS = (Q_COLS + K_COLS) // BLOCK
+
+X_CHUNKS = ((0, 1), (1, 3), (4, 4), (8, 8))
+TABLE_TILES = 4
+
+FREQ_STEP = 10000.0 ** (-2.0 / HEAD)
+TWO_PI = 2.0 * math.pi
+TURN_HI = 6.28125
+TURN_LO = TWO_PI - TURN_HI
+
+
+def load_codes(nc, tile_ap, words, g0, g1, b0, b1):
+    nc.sync.dma_start(
+        out=tile_ap.bitcast(I32),
+        in_=words[g0:g1, :, b0:b1].rearrange("g p n -> p g n").bitcast(I32),
+    )
+
+
+def load_scales(nc, plane, scales, c0, c1):
+    for q in range(4):
+        nc.sync.dma_start(
+            out=plane[32 * q : 32 * q + 4, :, :].bitcast(I32),
+            in_=scales[:, 4 * q : 4 * q + 4, c0:c1].rearrange("g r n -> r g n").bitcast(I32),
+        )
+
+
+def tile_groupedqueryattention_pa_kernel(
+    tc, x_words, x_scales, wq_words, wq_scales, wk_words, wk_scales, out_0, out_1
+):
+    nc = tc.nc
+    q_out = out_0.rearrange("b s h d -> (b s) (h d)")
+    k_out = out_1.rearrange("b s h d -> (b s) (h d)")
+
+    with ExitStack() as ctx:
+        keep = ctx.enter_context(tc.tile_pool(name="keep", bufs=1))
+        scratch = ctx.enter_context(tc.tile_pool(name="scratch", bufs=2))
+        work = ctx.enter_context(tc.tile_pool(name="work", bufs=3))
+        psum = ctx.enter_context(tc.psum_pool(name="psum", bufs=8))
+
+        xc = []
+        xs = []
+        for c, (t0, cnt) in enumerate(X_CHUNKS):
+            xc_tile = keep.tile([P, PASSES, 2 * P * cnt], U8, name="xc%d" % c, align_bytes=64)
+            xs_tile = keep.tile([P, PASSES, P * cnt], U8, name="xs%d" % c, align_bytes=64)
+            xc.append(xc_tile)
+            xs.append(xs_tile)
+        wc0a = keep.tile([P, 2, 2 * BLOCK], U8, name="wc0a", align_bytes=64)
+        wc0b = keep.tile([P, PASSES - 2, 2 * BLOCK], U8, name="wc0b", align_bytes=64)
+        wc = [None]
+        ws = []
+        for b in range(BLOCKS):
+            if b > 0:
+                wc_tile = keep.tile([P, PASSES, 2 * BLOCK], U8, name="wc%d" % b, align_bytes=64)
+                wc.append(wc_tile)
+            ws_tile = keep.tile([P, PASSES, BLOCK], U8, name="ws%d" % b, align_bytes=64)
+            ws.append(ws_tile)
+
+        def w_source(b):
+            if b < Q_BLOCKS:
+                return wq_words, wq_scales, b * BLOCK
+            return wk_words, wk_scales, (b - Q_BLOCKS) * BLOCK
+
+        def w_codes(b, g):
+            if b > 0:
+                return wc[b][:, g, :]
+            if g < 2:
+                return wc0a[:, g, :]
+            return wc0b[:, g - 2, :]
+
+        def x_place(t):
+            for c, (t0, cnt) in enumerate(X_CHUNKS):
+                if t0 <= t < t0 + cnt:
+                    return c, t - t0
+            raise ValueError("no chunk")
+
+        nc.vector.memset(xs[0][:].bitcast(I32), 0)
+        nc.vector.memset(ws[0][:].bitcast(I32), 0)
+        nc.vector.memset(xs[1][:].bitcast(I32), 0)
+        warm = keep.tile([P, 1], F32, name="warm")
+        nc.vector.memset(warm[:], 0.0)
+        nc.scalar.activation(out=warm[:], in_=warm[:], func=ACT.Sin)
+        pos = keep.tile([P, TOKEN_TILES], F32, name="pos")
+        nc.gpsimd.iota(
+            pos[:], pattern=[[P, TOKEN_TILES]], base=0, channel_multiplier=1,
+            allow_small_or_imprecise_dtypes=True,
+        )
+        nc.gpsimd.memset(xs[2][:].bitcast(F32), 0.0)
+        nc.gpsimd.memset(xs[3][:].bitcast(F32), 0.0)
+
+        load_codes(nc, wc0a[:], wq_words, 0, 2, 0, 2 * BLOCK)
+        load_codes(nc, xc[0][:], x_words, 0, PASSES, 0, 2 * P)
+        load_scales(nc, xs[0], x_scales, 0, P)
+        load_scales(nc, ws[0], wq_scales, 0, BLOCK)
+        load_codes(nc, wc0b[:], wq_words, 2, PASSES, 0, 2 * BLOCK)
+        for c in range(1, len(X_CHUNKS)):
+            t0, cnt = X_CHUNKS[c]
+            load_codes(nc, xc[c][:], x_words, 0, PASSES, 2 * P * t0, 2 * P * (t0 + cnt))
+            load_scales(nc, xs[c], x_scales, P * t0, P * (t0 + cnt))
+        for b in range(1, BLOCKS):
+            words, scales, c0 = w_source(b)
+            nc.gpsimd.memset(ws[b][:].bitcast(F32), 0.0)
+            load_scales(nc, ws[b], scales, c0, c0 + BLOCK)
+            load_codes(nc, wc[b][:], words, 0, PASSES, 2 * c0, 2 * (c0 + BLOCK))
+
+        freq = keep.tile([P, HALF], F32, name="freq")
+        nc.vector.memset(freq[:, 0:1], 1.0)
+        for k in range(7):
+            w = 2 ** k
+            nc.vector.tensor_scalar(
+                out=freq[:, w : 2 * w], in0=freq[:, 0:w], scalar1=FREQ_STEP ** w, scalar2=None, op0=ALU.mult
+            )
+        cos_t = []
+        sin_t = []
+        width = TABLE_TILES * HALF
+        for c in range(TOKEN_TILES // TABLE_TILES):
+            ang = scratch.tile([P, width], F32, name="ang")
+            for j in range(TABLE_TILES):
+                t = TABLE_TILES * c + j
+                nc.scalar.activation(
+                    out=ang[:, j * HALF : (j + 1) * HALF], in_=freq[:], func=ACT.Copy, scale=pos[:, t : t + 1]
+                )
+            turns = scratch.tile([P, width], I32, name="turns")
+            nc.vector.tensor_scalar(
+                out=turns[:], in0=ang[:], scalar1=1.0 / TWO_PI, scalar2=0.125, op0=ALU.mult, op1=ALU.add
+            )
+            red1 = scratch.tile([P, width], F32, name="red1")
+            nc.vector.scalar_tensor_tensor(
+                out=red1[:], in0=turns[:], scalar=-TURN_HI, in1=ang[:], op0=ALU.mult, op1=ALU.add
+            )
+            red = scratch.tile([P, width], F32, name="red")
+            nc.vector.scalar_tensor_tensor(
+                out=red[:], in0=turns[:], scalar=-TURN_LO, in1=red1[:], op0=ALU.mult, op1=ALU.add
+            )
+            shifted = scratch.tile([P, width], F32, name="shifted")
+            nc.gpsimd.tensor_scalar(
+                out=shifted[:], in0=red[:], scalar1=0.5, scalar2=-math.pi / 4.0, op0=ALU.mult, op1=ALU.add
+            )
+            sc = scratch.tile([P, width], F32, name="sc")
+            nc.scalar.activation(out=sc[:], in_=red[:], func=ACT.Sin, scale=0.5)
+            ss = scratch.tile([P, width], F32, name="ss")
+            nc.scalar.activation(out=ss[:], in_=shifted[:], func=ACT.Sin)
+            qc = scratch.tile([P, width], F32, name="qc")
+            nc.scalar.activation(out=qc[:], in_=sc[:], func=ACT.Square)
+            qs = scratch.tile([P, width], F32, name="qs")
+            nc.scalar.activation(out=qs[:], in_=ss[:], func=ACT.Square)
+            cos_c = keep.tile([P, TABLE_TILES, HALF], F32, name="cos%d" % c)
+            sin_c = keep.tile([P, TABLE_TILES, 2, HALF], F32, name="sin%d" % c)
+            nc.gpsimd.tensor_scalar(
+                out=cos_c[:], in0=qc[:].rearrange("p (j i) -> p j i", i=HALF),
+                scalar1=-2.0, scalar2=1.0, op0=ALU.mult, op1=ALU.add,
+            )
+            nc.gpsimd.tensor_scalar(
+                out=sin_c[:, :, 0, :], in0=qs[:].rearrange("p (j i) -> p j i", i=HALF),
+                scalar1=-2.0, scalar2=1.0, op0=ALU.mult, op1=ALU.add,
+            )
+            nc.gpsimd.tensor_scalar(
+                out=sin_c[:, :, 1, :], in0=qs[:].rearrange("p (j i) -> p j i", i=HALF),
+                scalar1=2.0, scalar2=-1.0, op0=ALU.mult, op1=ALU.add,
+            )
+            cos_t.append(cos_c)
+            sin_t.append(sin_c)
+
+        def project(b, t, n0, n1):
+            c, j = x_place(t)
+            acc = psum.tile([P, n1 - n0], F32, name="acc")
+            for g in range(PASSES):
+                nc.tensor.matmul_mx(
+                    out=acc[:],
+                    lhsT=xc[c][:, g, 2 * P * j : 2 * P * (j + 1)].bitcast(FP4X4),
+                    lhsT_scale=xs[c][:, g, P * j : P * (j + 1)],
+                    rhs=w_codes(b, g)[:, 2 * n0 : 2 * n1].bitcast(FP4X4),
+                    rhs_scale=ws[b][:, g, n0:n1],
+                    start=(g == 0),
+                    stop=(g == PASSES - 1),
+                )
+            return acc
+
+        def products(acc, t, heads):
+            c, j = divmod(t, TABLE_TILES)
+            by_cos = work.tile([P, heads, 2, HALF], F32, name="by_cos")
+            by_sin = work.tile([P, heads, 2, HALF], F32, name="by_sin")
+            nc.vector.tensor_tensor(
+                out=by_cos[:].rearrange("p h a i -> p (h a) i"),
+                in0=acc[:].rearrange("p (k i) -> p k i", i=HALF),
+                in1=cos_t[c][:, j : j + 1, :].to_broadcast([P, 2 * heads, HALF]),
+                op=ALU.mult,
+            )
+            nc.vector.tensor_tensor(
+                out=by_sin[:].rearrange("p h a i -> p h (a i)"),
+                in0=acc[:].rearrange("p (h k) -> p h k", k=HEAD),
+                in1=sin_t[c][:, j : j + 1, :, :].rearrange("p j a i -> p j (a i)").to_broadcast([P, heads, HEAD]),
+                op=ALU.mult,
+            )
+            return by_cos, by_sin
+
+        def combine(by_cos, by_sin, b, t, n0, heads):
+            y = work.tile([P, heads, 2, HALF], F32, name="y", bufs=4)
+            nc.vector.tensor_tensor(out=y[:, :, 0, :], in0=by_cos[:, :, 0, :], in1=by_sin[:, :, 1, :], op=ALU.add)
+            nc.vector.tensor_tensor(out=y[:, :, 1, :], in0=by_cos[:, :, 1, :], in1=by_sin[:, :, 0, :], op=ALU.add)
+            if b < Q_BLOCKS:
+                dst, c0 = q_out, b * BLOCK + n0
+            else:
+                dst, c0 = k_out, (b - Q_BLOCKS) * BLOCK + n0
+            nc.scalar.dma_start(
+                out=dst[t * P : (t + 1) * P, c0 : c0 + heads * HEAD],
+                in_=y[:].rearrange("p h a i -> p (h a i)"),
+            )
+
+        units = []
+        for b in range(BLOCKS):
+            for t in range(TOKEN_TILES):
+                if b == BLOCKS - 1 and t == TOKEN_TILES - 1:
+                    units.append((b, t, 0, HEAD))
+                    units.append((b, t, HEAD, BLOCK))
+                else:
+                    units.append((b, t, 0, BLOCK))
+
+        pending = None
+        for b, t, n0, n1 in units:
+            heads = (n1 - n0) // HEAD
+            acc = project(b, t, n0, n1)
+            by_cos, by_sin = products(acc, t, heads)
+            if pending is not None:
+                combine(*pending)
+            pending = (by_cos, by_sin, b, t, n0, heads)
+        combine(*pending)

@@ -121,7 +121,8 @@ def tile_groupedqueryattention_pa_kernel(
             t0, cnt = X_CHUNKS[c]
             load_codes(nc, xc[c][:], x_words, 0, PASSES, 2 * P * t0, 2 * P * (t0 + cnt))
             load_scales(nc, xs[c], x_scales, P * t0, P * (t0 + cnt))
-        for b in range(1, BLOCKS):
+
+        def load_block(b):
             words, scales, c0 = w_source(b)
             nc.gpsimd.memset(ws[b][:].bitcast(F32), 0.0)
             load_scales(nc, ws[b], scales, c0, c0 + BLOCK)
@@ -137,7 +138,8 @@ def tile_groupedqueryattention_pa_kernel(
         cos_t = []
         sin_t = []
         width = TABLE_TILES * HALF
-        for c in range(TOKEN_TILES // TABLE_TILES):
+
+        def build_tables(c):
             ang = scratch.tile([P, width], F32, name="ang")
             for j in range(TABLE_TILES):
                 t = TABLE_TILES * c + j
@@ -185,6 +187,8 @@ def tile_groupedqueryattention_pa_kernel(
             cos_t.append(cos_c)
             sin_t.append(sin_c)
 
+        build_tables(0)
+
         def project(b, t, n0, n1):
             c, j = x_place(t)
             acc = psum.tile([P, n1 - n0], F32, name="acc")
@@ -202,17 +206,19 @@ def tile_groupedqueryattention_pa_kernel(
 
         def products(acc, t, heads):
             c, j = divmod(t, TABLE_TILES)
+            x_sb = work.tile([P, heads * HEAD], F32, name="x_sb", bufs=4)
+            nc.scalar.copy(out=x_sb[:], in_=acc[:])
             by_cos = work.tile([P, heads, 2, HALF], F32, name="by_cos")
             by_sin = work.tile([P, heads, 2, HALF], F32, name="by_sin")
             nc.vector.tensor_tensor(
                 out=by_cos[:].rearrange("p h a i -> p (h a) i"),
-                in0=acc[:].rearrange("p (k i) -> p k i", i=HALF),
+                in0=x_sb[:].rearrange("p (k i) -> p k i", i=HALF),
                 in1=cos_t[c][:, j : j + 1, :].to_broadcast([P, 2 * heads, HALF]),
                 op=ALU.mult,
             )
             nc.vector.tensor_tensor(
                 out=by_sin[:].rearrange("p h a i -> p h (a i)"),
-                in0=acc[:].rearrange("p (h k) -> p h k", k=HEAD),
+                in0=x_sb[:].rearrange("p (h k) -> p h k", k=HEAD),
                 in1=sin_t[c][:, j : j + 1, :, :].rearrange("p j a i -> p j (a i)").to_broadcast([P, heads, HEAD]),
                 op=ALU.mult,
             )
@@ -226,7 +232,7 @@ def tile_groupedqueryattention_pa_kernel(
                 dst, c0 = q_out, b * BLOCK + n0
             else:
                 dst, c0 = k_out, (b - Q_BLOCKS) * BLOCK + n0
-            nc.scalar.dma_start(
+            nc.sync.dma_start(
                 out=dst[t * P : (t + 1) * P, c0 : c0 + heads * HEAD],
                 in_=y[:].rearrange("p h a i -> p (h a i)"),
             )
@@ -243,6 +249,10 @@ def tile_groupedqueryattention_pa_kernel(
         pending = None
         for b, t, n0, n1 in units:
             heads = (n1 - n0) // HEAD
+            if t == 0 and n0 == 0 and b + 1 < BLOCKS:
+                load_block(b + 1)
+            if b == 0 and t % TABLE_TILES == 1 and t // TABLE_TILES + 1 < TOKEN_TILES // TABLE_TILES:
+                build_tables(t // TABLE_TILES + 1)
             acc = project(b, t, n0, n1)
             by_cos, by_sin = products(acc, t, heads)
             if pending is not None:

@@ -6,6 +6,7 @@ import concourse.mybir as mybir
 F32 = mybir.dt.float32
 I32 = mybir.dt.int32
 U8 = mybir.dt.uint8
+BF16 = mybir.dt.bfloat16
 FP4X4 = mybir.dt.float4_e2m1fn_x4
 ALU = mybir.AluOpType
 ACT = mybir.ActivationFunctionType
@@ -27,6 +28,7 @@ BLOCKS = (Q_COLS + K_COLS) // BLOCK
 
 X_CHUNKS = ((0, 1), (1, 3), (4, 4), (8, 8))
 TABLE_TILES = 4
+WARM_MATMULS = 14
 
 FREQ_STEP = 10000.0 ** (-2.0 / HEAD)
 TWO_PI = 2.0 * math.pi
@@ -98,6 +100,11 @@ def tile_groupedqueryattention_pa_kernel(
                     return c, t - t0
             raise ValueError("no chunk")
 
+        zeros = keep.tile([P, BLOCK], BF16, name="zeros")
+        nc.gpsimd.memset(zeros[:], 0.0)
+        warm_acc = psum.tile([P, BLOCK], F32, name="acc")
+        for i in range(WARM_MATMULS):
+            nc.tensor.matmul(out=warm_acc[:], lhsT=zeros[:, 0:P], rhs=zeros[:], start=True, stop=True)
         nc.vector.memset(xs[0][:].bitcast(I32), 0)
         nc.vector.memset(ws[0][:].bitcast(I32), 0)
         nc.vector.memset(xs[1][:].bitcast(I32), 0)
@@ -204,10 +211,13 @@ def tile_groupedqueryattention_pa_kernel(
                 )
             return acc
 
-        def products(acc, t, heads):
+        def products(acc, t, heads, last):
             c, j = divmod(t, TABLE_TILES)
-            x_sb = work.tile([P, heads * HEAD], F32, name="x_sb", bufs=4)
-            nc.scalar.copy(out=x_sb[:], in_=acc[:])
+            if last:
+                x_sb = acc
+            else:
+                x_sb = work.tile([P, heads * HEAD], F32, name="x_sb", bufs=4)
+                nc.scalar.copy(out=x_sb[:], in_=acc[:])
             by_cos = work.tile([P, heads, 2, HALF], F32, name="by_cos")
             by_sin = work.tile([P, heads, 2, HALF], F32, name="by_sin")
             nc.vector.tensor_tensor(
@@ -254,7 +264,7 @@ def tile_groupedqueryattention_pa_kernel(
             if b == 0 and t % TABLE_TILES == 1 and t // TABLE_TILES + 1 < TOKEN_TILES // TABLE_TILES:
                 build_tables(t // TABLE_TILES + 1)
             acc = project(b, t, n0, n1)
-            by_cos, by_sin = products(acc, t, heads)
+            by_cos, by_sin = products(acc, t, heads, (b, t, n0, n1) == units[-1])
             if pending is not None:
                 combine(*pending)
             pending = (by_cos, by_sin, b, t, n0, heads)

@@ -6,7 +6,6 @@ import concourse.mybir as mybir
 F32 = mybir.dt.float32
 I32 = mybir.dt.int32
 U8 = mybir.dt.uint8
-BF16 = mybir.dt.bfloat16
 FP4X4 = mybir.dt.float4_e2m1fn_x4
 ALU = mybir.AluOpType
 ACT = mybir.ActivationFunctionType
@@ -28,7 +27,6 @@ BLOCKS = (Q_COLS + K_COLS) // BLOCK
 
 X_CHUNKS = ((0, 1), (1, 3), (4, 4), (8, 8))
 TABLE_TILES = 4
-WARM_MATMULS = 14
 
 FREQ_STEP = 10000.0 ** (-2.0 / HEAD)
 TWO_PI = 2.0 * math.pi
@@ -100,11 +98,6 @@ def tile_groupedqueryattention_pa_kernel(
                     return c, t - t0
             raise ValueError("no chunk")
 
-        zeros = keep.tile([P, BLOCK], BF16, name="zeros")
-        nc.gpsimd.memset(zeros[:], 0.0)
-        warm_acc = psum.tile([P, BLOCK], F32, name="acc")
-        for i in range(WARM_MATMULS):
-            nc.tensor.matmul(out=warm_acc[:], lhsT=zeros[:, 0:P], rhs=zeros[:], start=True, stop=True)
         nc.vector.memset(xs[0][:].bitcast(I32), 0)
         nc.vector.memset(ws[0][:].bitcast(I32), 0)
         nc.vector.memset(xs[1][:].bitcast(I32), 0)
@@ -211,13 +204,9 @@ def tile_groupedqueryattention_pa_kernel(
                 )
             return acc
 
-        def products(acc, t, heads, last):
+        def products(acc, t, heads):
             c, j = divmod(t, TABLE_TILES)
-            if last:
-                x_sb = acc
-            else:
-                x_sb = work.tile([P, heads * HEAD], F32, name="x_sb", bufs=4)
-                nc.scalar.copy(out=x_sb[:], in_=acc[:])
+            x_sb = acc
             by_cos = work.tile([P, heads, 2, HALF], F32, name="by_cos")
             by_sin = work.tile([P, heads, 2, HALF], F32, name="by_sin")
             nc.vector.tensor_tensor(
@@ -264,7 +253,7 @@ def tile_groupedqueryattention_pa_kernel(
             if b == 0 and t % TABLE_TILES == 1 and t // TABLE_TILES + 1 < TOKEN_TILES // TABLE_TILES:
                 build_tables(t // TABLE_TILES + 1)
             acc = project(b, t, n0, n1)
-            by_cos, by_sin = products(acc, t, heads, (b, t, n0, n1) == units[-1])
+            by_cos, by_sin = products(acc, t, heads)
             if pending is not None:
                 combine(*pending)
             pending = (by_cos, by_sin, b, t, n0, heads)

@@ -25,7 +25,8 @@ HEAD = 2 * HALF
 Q_BLOCKS = Q_COLS // BLOCK
 BLOCKS = (Q_COLS + K_COLS) // BLOCK
 
-X_CHUNKS = ((0, 1), (1, 3), (4, 4), (8, 8))
+X_CHUNKS = ((0, 1), (1, 3), (4, 4), (8, 4), (12, 4))
+LEAD = 10
 TABLE_TILES = 4
 
 FREQ_STEP = 10000.0 ** (-2.0 / HEAD)
@@ -61,6 +62,7 @@ def tile_groupedqueryattention_pa_kernel(
         scratch = ctx.enter_context(tc.tile_pool(name="scratch", bufs=2))
         work = ctx.enter_context(tc.tile_pool(name="work", bufs=3))
         psum = ctx.enter_context(tc.psum_pool(name="psum", bufs=8))
+        ctx.enter_context(tc.manual_schedule())
 
         xc = []
         xs = []
@@ -109,18 +111,21 @@ def tile_groupedqueryattention_pa_kernel(
             pos[:], pattern=[[P, TOKEN_TILES]], base=0, channel_multiplier=1,
             allow_small_or_imprecise_dtypes=True,
         )
-        nc.gpsimd.memset(xs[2][:].bitcast(F32), 0.0)
-        nc.gpsimd.memset(xs[3][:].bitcast(F32), 0.0)
 
         load_codes(nc, wc0a[:], wq_words, 0, 2, 0, 2 * BLOCK)
         load_codes(nc, xc[0][:], x_words, 0, PASSES, 0, 2 * P)
         load_scales(nc, xs[0], x_scales, 0, P)
         load_scales(nc, ws[0], wq_scales, 0, BLOCK)
         load_codes(nc, wc0b[:], wq_words, 2, PASSES, 0, 2 * BLOCK)
-        for c in range(1, len(X_CHUNKS)):
+
+        def load_chunk(c):
             t0, cnt = X_CHUNKS[c]
+            if c > 1:
+                nc.gpsimd.memset(xs[c][:].bitcast(F32), 0.0)
             load_codes(nc, xc[c][:], x_words, 0, PASSES, 2 * P * t0, 2 * P * (t0 + cnt))
             load_scales(nc, xs[c], x_scales, P * t0, P * (t0 + cnt))
+
+        load_chunk(1)
 
         def load_block(b):
             words, scales, c0 = w_source(b)
@@ -187,8 +192,6 @@ def tile_groupedqueryattention_pa_kernel(
             cos_t.append(cos_c)
             sin_t.append(sin_c)
 
-        build_tables(0)
-
         def project(b, t, n0, n1):
             c, j = x_place(t)
             acc = psum.tile([P, n1 - n0], F32, name="acc")
@@ -237,21 +240,49 @@ def tile_groupedqueryattention_pa_kernel(
             )
 
         units = []
-        for b in range(BLOCKS):
-            for t in range(TOKEN_TILES):
-                if b == BLOCKS - 1 and t == TOKEN_TILES - 1:
-                    units.append((b, t, 0, HEAD))
-                    units.append((b, t, HEAD, BLOCK))
-                else:
-                    units.append((b, t, 0, BLOCK))
+        hooks = {}
+
+        def at(index, what, arg):
+            hooks.setdefault(max(index, 0), []).append((what, arg))
+
+        blocks_in = 1
+        tiles_in = 4
+        for t in range(tiles_in):
+            units.append((0, t))
+        while blocks_in < BLOCKS or tiles_in < TOKEN_TILES:
+            if blocks_in < BLOCKS:
+                at(len(units) - LEAD, "block", blocks_in)
+                for t in range(tiles_in):
+                    units.append((blocks_in, t))
+                blocks_in += 1
+            if tiles_in < TOKEN_TILES:
+                at(len(units) - LEAD, "chunk", tiles_in // 4 + 1)
+                at(len(units) - 5, "tables", tiles_in // TABLE_TILES)
+                for t in range(tiles_in, tiles_in + 4):
+                    for b in range(blocks_in):
+                        units.append((b, t))
+                tiles_in += 4
+        at(0, "tables", 0)
+
+        pieces = []
+        for index, (b, t) in enumerate(units):
+            if index == len(units) - 1:
+                pieces.append((index, b, t, 0, HEAD))
+                pieces.append((index, b, t, HEAD, BLOCK))
+            else:
+                pieces.append((index, b, t, 0, BLOCK))
 
         pending = None
-        for b, t, n0, n1 in units:
+        for index, b, t, n0, n1 in pieces:
             heads = (n1 - n0) // HEAD
-            if t == 0 and n0 == 0 and b + 1 < BLOCKS:
-                load_block(b + 1)
-            if b == 0 and t % TABLE_TILES == 1 and t // TABLE_TILES + 1 < TOKEN_TILES // TABLE_TILES:
-                build_tables(t // TABLE_TILES + 1)
+            if n0 == 0:
+                for what, arg in hooks.get(index, []):
+                    if what == "block":
+                        load_block(arg)
+                    elif what == "chunk":
+                        load_chunk(arg)
+                    else:
+                        build_tables(arg)
             acc = project(b, t, n0, n1)
             by_cos, by_sin = products(acc, t, heads)
             if pending is not None:

@@ -43,10 +43,10 @@ def load_codes(nc, tile_ap, words, g0, g1, b0, b1):
 
 
 def load_scales(nc, plane, scales, c0, c1):
-    for q in range(4):
+    for r in range(4):
         nc.sync.dma_start(
-            out=plane[32 * q : 32 * q + 4, :, :].bitcast(I32),
-            in_=scales[:, 4 * q : 4 * q + 4, c0:c1].rearrange("g r n -> r g n").bitcast(I32),
+            out=plane[r : P : 32, :, :].bitcast(I32),
+            in_=scales[:, r : 16 : 4, c0:c1].rearrange("g q n -> q g n").bitcast(I32),
         )
 
 

@@ -25,7 +25,10 @@ HEAD = 2 * HALF
 Q_BLOCKS = Q_COLS // BLOCK
 BLOCKS = (Q_COLS + K_COLS) // BLOCK
 
-X_CHUNKS = ((0, 1), (1, 3), (4, 4), (8, 4), (12, 4))
+GROUP = 4
+X_CHUNKS = TOKEN_TILES // GROUP
+FIRST_RANGES = ((0, 2), (2, 2), (4, 4))
+WHOLE_RANGE = ((0, PASSES),)
 LEAD = 10
 TABLE_TILES = 4
 
@@ -64,21 +67,29 @@ def tile_groupedqueryattention_pa_kernel(
         psum = ctx.enter_context(tc.psum_pool(name="psum", bufs=8))
         ctx.enter_context(tc.manual_schedule())
 
+        def code_tiles(name, width, ranges):
+            parts = []
+            for g0, cnt in ranges:
+                part = keep.tile([P, cnt, width], U8, name="%s_%d" % (name, g0), align_bytes=64)
+                parts.append((g0, cnt, part))
+            return parts
+
+        def code_pass(parts, g):
+            for g0, cnt, part in parts:
+                if g0 <= g < g0 + cnt:
+                    return part[:, g - g0, :]
+            raise ValueError("no such pass")
+
         xc = []
         xs = []
-        for c, (t0, cnt) in enumerate(X_CHUNKS):
-            xc_tile = keep.tile([P, PASSES, 2 * P * cnt], U8, name="xc%d" % c, align_bytes=64)
-            xs_tile = keep.tile([P, PASSES, P * cnt], U8, name="xs%d" % c, align_bytes=64)
-            xc.append(xc_tile)
+        for c in range(X_CHUNKS):
+            xc.append(code_tiles("xc%d" % c, 2 * P * GROUP, FIRST_RANGES if c == 0 else WHOLE_RANGE))
+            xs_tile = keep.tile([P, PASSES, P * GROUP], U8, name="xs%d" % c, align_bytes=64)
             xs.append(xs_tile)
-        wc0a = keep.tile([P, 2, 2 * BLOCK], U8, name="wc0a", align_bytes=64)
-        wc0b = keep.tile([P, PASSES - 2, 2 * BLOCK], U8, name="wc0b", align_bytes=64)
-        wc = [None]
+        wc = []
         ws = []
         for b in range(BLOCKS):
-            if b > 0:
-                wc_tile = keep.tile([P, PASSES, 2 * BLOCK], U8, name="wc%d" % b, align_bytes=64)
-                wc.append(wc_tile)
+            wc.append(code_tiles("wc%d" % b, 2 * BLOCK, FIRST_RANGES if b == 0 else WHOLE_RANGE))
             ws_tile = keep.tile([P, PASSES, BLOCK], U8, name="ws%d" % b, align_bytes=64)
             ws.append(ws_tile)
 
@@ -87,22 +98,8 @@ def tile_groupedqueryattention_pa_kernel(
                 return wq_words, wq_scales, b * BLOCK
             return wk_words, wk_scales, (b - Q_BLOCKS) * BLOCK
 
-        def w_codes(b, g):
-            if b > 0:
-                return wc[b][:, g, :]
-            if g < 2:
-                return wc0a[:, g, :]
-            return wc0b[:, g - 2, :]
-
-        def x_place(t):
-            for c, (t0, cnt) in enumerate(X_CHUNKS):
-                if t0 <= t < t0 + cnt:
-                    return c, t - t0
-            raise ValueError("no chunk")
-
         nc.vector.memset(xs[0][:].bitcast(I32), 0)
-        nc.vector.memset(ws[0][:].bitcast(I32), 0)
-        nc.vector.memset(xs[1][:].bitcast(I32), 0)
+        nc.gpsimd.memset(ws[0][:].bitcast(F32), 0.0)
         warm = keep.tile([P, 1], F32, name="warm")
         nc.vector.memset(warm[:], 0.0)
         nc.scalar.activation(out=warm[:], in_=warm[:], func=ACT.Sin)
@@ -112,26 +109,28 @@ def tile_groupedqueryattention_pa_kernel(
             allow_small_or_imprecise_dtypes=True,
         )
 
-        load_codes(nc, wc0a[:], wq_words, 0, 2, 0, 2 * BLOCK)
-        load_codes(nc, xc[0][:], x_words, 0, PASSES, 0, 2 * P)
-        load_scales(nc, xs[0], x_scales, 0, P)
-        load_scales(nc, ws[0], wq_scales, 0, BLOCK)
-        load_codes(nc, wc0b[:], wq_words, 2, PASSES, 0, 2 * BLOCK)
+        for i in range(len(FIRST_RANGES)):
+            g0, cnt, part = xc[0][i]
+            load_codes(nc, part[:], x_words, g0, g0 + cnt, 0, 2 * P * GROUP)
+            g0, cnt, part = wc[0][i]
+            load_codes(nc, part[:], wq_words, g0, g0 + cnt, 0, 2 * BLOCK)
+            if i == 0:
+                load_scales(nc, ws[0], wq_scales, 0, BLOCK)
+                load_scales(nc, xs[0], x_scales, 0, P * GROUP)
 
         def load_chunk(c):
-            t0, cnt = X_CHUNKS[c]
-            if c > 1:
-                nc.gpsimd.memset(xs[c][:].bitcast(F32), 0.0)
-            load_codes(nc, xc[c][:], x_words, 0, PASSES, 2 * P * t0, 2 * P * (t0 + cnt))
-            load_scales(nc, xs[c], x_scales, P * t0, P * (t0 + cnt))
-
-        load_chunk(1)
+            c0 = P * GROUP * c
+            nc.gpsimd.memset(xs[c][:].bitcast(F32), 0.0)
+            g0, cnt, part = xc[c][0]
+            load_codes(nc, part[:], x_words, 0, PASSES, 2 * c0, 2 * (c0 + P * GROUP))
+            load_scales(nc, xs[c], x_scales, c0, c0 + P * GROUP)
 
         def load_block(b):
             words, scales, c0 = w_source(b)
             nc.gpsimd.memset(ws[b][:].bitcast(F32), 0.0)
             load_scales(nc, ws[b], scales, c0, c0 + BLOCK)
-            load_codes(nc, wc[b][:], words, 0, PASSES, 2 * c0, 2 * (c0 + BLOCK))
+            g0, cnt, part = wc[b][0]
+            load_codes(nc, part[:], words, 0, PASSES, 2 * c0, 2 * (c0 + BLOCK))
 
         freq = keep.tile([P, HALF], F32, name="freq")
         nc.vector.memset(freq[:, 0:1], 1.0)
@@ -192,19 +191,22 @@ def tile_groupedqueryattention_pa_kernel(
             cos_t.append(cos_c)
             sin_t.append(sin_c)
 
+        def one_pass(acc, b, t, n0, n1, g):
+            c, j = divmod(t, GROUP)
+            nc.tensor.matmul_mx(
+                out=acc[:],
+                lhsT=code_pass(xc[c], g)[:, 2 * P * j : 2 * P * (j + 1)].bitcast(FP4X4),
+                lhsT_scale=xs[c][:, g, P * j : P * (j + 1)],
+                rhs=code_pass(wc[b], g)[:, 2 * n0 : 2 * n1].bitcast(FP4X4),
+                rhs_scale=ws[b][:, g, n0:n1],
+                start=(g == 0),
+                stop=(g == PASSES - 1),
+            )
+
         def project(b, t, n0, n1):
-            c, j = x_place(t)
             acc = psum.tile([P, n1 - n0], F32, name="acc")
             for g in range(PASSES):
-                nc.tensor.matmul_mx(
-                    out=acc[:],
-                    lhsT=xc[c][:, g, 2 * P * j : 2 * P * (j + 1)].bitcast(FP4X4),
-                    lhsT_scale=xs[c][:, g, P * j : P * (j + 1)],
-                    rhs=w_codes(b, g)[:, 2 * n0 : 2 * n1].bitcast(FP4X4),
-                    rhs_scale=ws[b][:, g, n0:n1],
-                    start=(g == 0),
-                    stop=(g == PASSES - 1),
-                )
+                one_pass(acc, b, t, n0, n1, g)
             return acc
 
         def products(acc, t, heads):
@@ -246,7 +248,7 @@ def tile_groupedqueryattention_pa_kernel(
             hooks.setdefault(max(index, 0), []).append((what, arg))
 
         blocks_in = 1
-        tiles_in = 4
+        tiles_in = GROUP
         for t in range(tiles_in):
             units.append((0, t))
         while blocks_in < BLOCKS or tiles_in < TOKEN_TILES:
@@ -256,12 +258,12 @@ def tile_groupedqueryattention_pa_kernel(
                     units.append((blocks_in, t))
                 blocks_in += 1
             if tiles_in < TOKEN_TILES:
-                at(len(units) - LEAD, "chunk", tiles_in // 4 + 1)
+                at(len(units) - LEAD, "chunk", tiles_in // GROUP)
                 at(len(units) - 5, "tables", tiles_in // TABLE_TILES)
-                for t in range(tiles_in, tiles_in + 4):
+                for t in range(tiles_in, tiles_in + GROUP):
                     for b in range(blocks_in):
                         units.append((b, t))
-                tiles_in += 4
+                tiles_in += GROUP
         at(0, "tables", 0)
 
         pieces = []
@@ -272,18 +274,33 @@ def tile_groupedqueryattention_pa_kernel(
             else:
                 pieces.append((index, b, t, 0, BLOCK))
 
+        def run_hooks(index):
+            for what, arg in hooks.get(index, []):
+                if what == "block":
+                    load_block(arg)
+                elif what == "chunk":
+                    load_chunk(arg)
+                else:
+                    build_tables(arg)
+
+        first = []
+        for index in range(GROUP):
+            run_hooks(index)
+            acc = psum.tile([P, BLOCK], F32, name="acc")
+            first.append(acc)
+        for g in range(PASSES):
+            for t in range(GROUP):
+                one_pass(first[t], 0, t, 0, BLOCK, g)
+
         pending = None
         for index, b, t, n0, n1 in pieces:
             heads = (n1 - n0) // HEAD
-            if n0 == 0:
-                for what, arg in hooks.get(index, []):
-                    if what == "block":
-                        load_block(arg)
-                    elif what == "chunk":
-                        load_chunk(arg)
-                    else:
-                        build_tables(arg)
-            acc = project(b, t, n0, n1)
+            if index < GROUP:
+                acc = first[index]
+            else:
+                if n0 == 0:
+                    run_hooks(index)
+                acc = project(b, t, n0, n1)
             by_cos, by_sin = products(acc, t, heads)
             if pending is not None:
                 combine(*pending)

@@ -4,6 +4,7 @@ from contextlib import ExitStack
 import concourse.mybir as mybir
 
 F32 = mybir.dt.float32
+BF16 = mybir.dt.bfloat16
 I32 = mybir.dt.int32
 U8 = mybir.dt.uint8
 FP4X4 = mybir.dt.float4_e2m1fn_x4
@@ -30,6 +31,7 @@ X_CHUNKS = TOKEN_TILES // GROUP
 FIRST_RANGES = ((0, 2), (2, 2), (4, 4))
 WHOLE_RANGE = ((0, PASSES),)
 LEAD = 10
+WARM_UP = 14
 TABLE_TILES = 4
 
 FREQ_STEP = 10000.0 ** (-2.0 / HEAD)
@@ -97,6 +99,12 @@ def tile_groupedqueryattention_pa_kernel(
             if b < Q_BLOCKS:
                 return wq_words, wq_scales, b * BLOCK
             return wk_words, wk_scales, (b - Q_BLOCKS) * BLOCK
+
+        zero = keep.tile([P, BLOCK], BF16, name="zero")
+        nc.vector.memset(zero[:], 0.0)
+        junk = psum.tile([P, BLOCK], F32, name="acc")
+        for i in range(WARM_UP):
+            nc.tensor.matmul(out=junk[:], lhsT=zero[:, 0:P], rhs=zero[:], start=True, stop=True)
 
         nc.vector.memset(xs[0][:].bitcast(I32), 0)
         nc.gpsimd.memset(ws[0][:].bitcast(F32), 0.0)
@@ -230,8 +238,7 @@ def tile_groupedqueryattention_pa_kernel(
 
         def combine(by_cos, by_sin, b, t, n0, heads):
             y = work.tile([P, heads, 2, HALF], F32, name="y", bufs=4)
-            nc.vector.tensor_tensor(out=y[:, :, 0, :], in0=by_cos[:, :, 0, :], in1=by_sin[:, :, 1, :], op=ALU.add)
-            nc.vector.tensor_tensor(out=y[:, :, 1, :], in0=by_cos[:, :, 1, :], in1=by_sin[:, :, 0, :], op=ALU.add)
+            nc.vector.tensor_tensor(out=y[:], in0=by_cos[:], in1=by_sin[:, :, ::-1, :], op=ALU.add)
             if b < Q_BLOCKS:
                 dst, c0 = q_out, b * BLOCK + n0
             else:
@@ -268,7 +275,7 @@ def tile_groupedqueryattention_pa_kernel(
 
         pieces = []
         for index, (b, t) in enumerate(units):
-            if index == len(units) - 1:
+            if index >= len(units) - 2:
                 pieces.append((index, b, t, 0, HEAD))
                 pieces.append((index, b, t, HEAD, BLOCK))
             else:
@@ -293,7 +300,7 @@ def tile_groupedqueryattention_pa_kernel(
                 one_pass(first[t], 0, t, 0, BLOCK, g)
 
         pending = None
-        for index, b, t, n0, n1 in pieces:
+        for place, (index, b, t, n0, n1) in enumerate(pieces):
             heads = (n1 - n0) // HEAD
             if index < GROUP:
                 acc = first[index]
@@ -301,6 +308,9 @@ def tile_groupedqueryattention_pa_kernel(
                 if n0 == 0:
                     run_hooks(index)
                 acc = project(b, t, n0, n1)
+            if place == len(pieces) - 1:
+                combine(*pending)
+                pending = None
             by_cos, by_sin = products(acc, t, heads)
             if pending is not None:
                 combine(*pending)

@@ -28,10 +28,10 @@ BLOCKS = (Q_COLS + K_COLS) // BLOCK
 
 GROUP = 4
 X_CHUNKS = TOKEN_TILES // GROUP
-FIRST_RANGES = ((0, 2), (2, 2), (4, 4))
+FIRST_RANGES = ((0, 1), (1, 1), (2, 2), (4, 4))
 WHOLE_RANGE = ((0, PASSES),)
 LEAD = 10
-WARM_UP = 14
+WARM_UP = 12
 TABLE_TILES = 4
 
 FREQ_STEP = 10000.0 ** (-2.0 / HEAD)

@@ -106,8 +106,8 @@ def tile_groupedqueryattention_pa_kernel(
         for i in range(WARM_UP):
             nc.tensor.matmul(out=junk[:], lhsT=zero[:, 0:P], rhs=zero[:], start=True, stop=True)
 
+        nc.vector.memset(ws[0][:].bitcast(I32), 0)
         nc.vector.memset(xs[0][:].bitcast(I32), 0)
-        nc.gpsimd.memset(ws[0][:].bitcast(F32), 0.0)
         warm = keep.tile([P, 1], F32, name="warm")
         nc.vector.memset(warm[:], 0.0)
         nc.scalar.activation(out=warm[:], in_=warm[:], func=ACT.Sin)
@@ -126,16 +126,22 @@ def tile_groupedqueryattention_pa_kernel(
                 load_scales(nc, ws[0], wq_scales, 0, BLOCK)
                 load_scales(nc, xs[0], x_scales, 0, P * GROUP)
 
+        def zero_plane(plane, early):
+            if early:
+                nc.vector.memset(plane[:].bitcast(I32), 0)
+            else:
+                nc.gpsimd.memset(plane[:].bitcast(F32), 0.0)
+
         def load_chunk(c):
             c0 = P * GROUP * c
-            nc.gpsimd.memset(xs[c][:].bitcast(F32), 0.0)
+            zero_plane(xs[c], c == 1)
             g0, cnt, part = xc[c][0]
             load_codes(nc, part[:], x_words, 0, PASSES, 2 * c0, 2 * (c0 + P * GROUP))
             load_scales(nc, xs[c], x_scales, c0, c0 + P * GROUP)
 
         def load_block(b):
             words, scales, c0 = w_source(b)
-            nc.gpsimd.memset(ws[b][:].bitcast(F32), 0.0)
+            zero_plane(ws[b], b == 1)
             load_scales(nc, ws[b], scales, c0, c0 + BLOCK)
             g0, cnt, part = wc[b][0]
             load_codes(nc, part[:], words, 0, PASSES, 2 * c0, 2 * (c0 + BLOCK))

import math
from contextlib import ExitStack

import concourse.mybir as mybir

F32 = mybir.dt.float32
BF16 = mybir.dt.bfloat16
I32 = mybir.dt.int32
U8 = mybir.dt.uint8
FP4X4 = mybir.dt.float4_e2m1fn_x4
ALU = mybir.AluOpType
ACT = mybir.ActivationFunctionType

TOKENS = 2048
FEATURES = 4096
Q_COLS = 2048
K_COLS = 1024
FLOPS = 2 * TOKENS * FEATURES * (Q_COLS + K_COLS)

P = 128
PASSES = FEATURES // 512
TOKEN_TILES = TOKENS // P
BLOCK = 512
HALF = 128
HEAD = 2 * HALF
Q_BLOCKS = Q_COLS // BLOCK
BLOCKS = (Q_COLS + K_COLS) // BLOCK

GROUP = 4
X_CHUNKS = TOKEN_TILES // GROUP
FIRST_RANGES = ((0, 1), (1, 1), (2, 2), (4, 4))
WHOLE_RANGE = ((0, PASSES),)
LEAD = 10
WARM_UP = 12
TABLE_TILES = 4

FREQ_STEP = 10000.0 ** (-2.0 / HEAD)
TWO_PI = 2.0 * math.pi
TURN_HI = 6.28125
TURN_LO = TWO_PI - TURN_HI


def load_codes(nc, tile_ap, words, g0, g1, b0, b1):
    nc.sync.dma_start(
        out=tile_ap.bitcast(I32),
        in_=words[g0:g1, :, b0:b1].rearrange("g p n -> p g n").bitcast(I32),
    )


def load_scales(nc, plane, scales, c0, c1):
    for r in range(4):
        nc.sync.dma_start(
            out=plane[r : P : 32, :, :].bitcast(I32),
            in_=scales[:, r : 16 : 4, c0:c1].rearrange("g q n -> q g n").bitcast(I32),
        )


def tile_groupedqueryattention_pa_kernel(
    tc, x_words, x_scales, wq_words, wq_scales, wk_words, wk_scales, out_0, out_1
):
    nc = tc.nc
    q_out = out_0.rearrange("b s h d -> (b s) (h d)")
    k_out = out_1.rearrange("b s h d -> (b s) (h d)")

    with ExitStack() as ctx:
        keep = ctx.enter_context(tc.tile_pool(name="keep", bufs=1))
        scratch = ctx.enter_context(tc.tile_pool(name="scratch", bufs=2))
        work = ctx.enter_context(tc.tile_pool(name="work", bufs=3))
        psum = ctx.enter_context(tc.psum_pool(name="psum", bufs=8))
        ctx.enter_context(tc.manual_schedule())

        def code_tiles(name, width, ranges):
            parts = []
            for g0, cnt in ranges:
                part = keep.tile([P, cnt, width], U8, name="%s_%d" % (name, g0), align_bytes=64)
                parts.append((g0, cnt, part))
            return parts

        def code_pass(parts, g):
            for g0, cnt, part in parts:
                if g0 <= g < g0 + cnt:
                    return part[:, g - g0, :]
            raise ValueError("no such pass")

        xc = []
        xs = []
        for c in range(X_CHUNKS):
            xc.append(code_tiles("xc%d" % c, 2 * P * GROUP, FIRST_RANGES if c == 0 else WHOLE_RANGE))
            xs_tile = keep.tile([P, PASSES, P * GROUP], U8, name="xs%d" % c, align_bytes=64)
            xs.append(xs_tile)
        wc = []
        ws = []
        for b in range(BLOCKS):
            wc.append(code_tiles("wc%d" % b, 2 * BLOCK, FIRST_RANGES if b == 0 else WHOLE_RANGE))
            ws_tile = keep.tile([P, PASSES, BLOCK], U8, name="ws%d" % b, align_bytes=64)
            ws.append(ws_tile)

        def w_source(b):
            if b < Q_BLOCKS:
                return wq_words, wq_scales, b * BLOCK
            return wk_words, wk_scales, (b - Q_BLOCKS) * BLOCK

        zero = keep.tile([P, BLOCK], BF16, name="zero")
        nc.vector.memset(zero[:], 0.0)
        junk = psum.tile([P, BLOCK], F32, name="acc")
        for i in range(WARM_UP):
            nc.tensor.matmul(out=junk[:], lhsT=zero[:, 0:P], rhs=zero[:], start=True, stop=True)

        nc.vector.memset(ws[0][:].bitcast(I32), 0)
        nc.vector.memset(xs[0][:].bitcast(I32), 0)
        warm = keep.tile([P, 1], F32, name="warm")
        nc.vector.memset(warm[:], 0.0)
        nc.scalar.activation(out=warm[:], in_=warm[:], func=ACT.Sin)
        pos = keep.tile([P, TOKEN_TILES], F32, name="pos")
        nc.gpsimd.iota(
            pos[:], pattern=[[P, TOKEN_TILES]], base=0, channel_multiplier=1,
            allow_small_or_imprecise_dtypes=True,
        )

        for i in range(len(FIRST_RANGES)):
            g0, cnt, part = xc[0][i]
            load_codes(nc, part[:], x_words, g0, g0 + cnt, 0, 2 * P * GROUP)
            g0, cnt, part = wc[0][i]
            load_codes(nc, part[:], wq_words, g0, g0 + cnt, 0, 2 * BLOCK)
            if i == 0:
                load_scales(nc, ws[0], wq_scales, 0, BLOCK)
                load_scales(nc, xs[0], x_scales, 0, P * GROUP)

        def zero_plane(plane, early):
            if early:
                nc.vector.memset(plane[:].bitcast(I32), 0)
            else:
                nc.gpsimd.memset(plane[:].bitcast(F32), 0.0)

        def load_chunk(c):
            c0 = P * GROUP * c
            zero_plane(xs[c], c == 1)
            g0, cnt, part = xc[c][0]
            load_codes(nc, part[:], x_words, 0, PASSES, 2 * c0, 2 * (c0 + P * GROUP))
            load_scales(nc, xs[c], x_scales, c0, c0 + P * GROUP)

        def load_block(b):
            words, scales, c0 = w_source(b)
            zero_plane(ws[b], b == 1)
            load_scales(nc, ws[b], scales, c0, c0 + BLOCK)
            g0, cnt, part = wc[b][0]
            load_codes(nc, part[:], words, 0, PASSES, 2 * c0, 2 * (c0 + BLOCK))

        freq = keep.tile([P, HALF], F32, name="freq")
        nc.vector.memset(freq[:, 0:1], 1.0)
        for k in range(7):
            w = 2 ** k
            nc.vector.tensor_scalar(
                out=freq[:, w : 2 * w], in0=freq[:, 0:w], scalar1=FREQ_STEP ** w, scalar2=None, op0=ALU.mult
            )
        cos_t = []
        sin_t = []
        width = TABLE_TILES * HALF

        def build_tables(c):
            ang = scratch.tile([P, width], F32, name="ang")
            for j in range(TABLE_TILES):
                t = TABLE_TILES * c + j
                nc.scalar.activation(
                    out=ang[:, j * HALF : (j + 1) * HALF], in_=freq[:], func=ACT.Copy, scale=pos[:, t : t + 1]
                )
            turns = scratch.tile([P, width], I32, name="turns")
            nc.vector.tensor_scalar(
                out=turns[:], in0=ang[:], scalar1=1.0 / TWO_PI, scalar2=0.125, op0=ALU.mult, op1=ALU.add
            )
            red1 = scratch.tile([P, width], F32, name="red1")
            nc.vector.scalar_tensor_tensor(
                out=red1[:], in0=turns[:], scalar=-TURN_HI, in1=ang[:], op0=ALU.mult, op1=ALU.add
            )
            red = scratch.tile([P, width], F32, name="red")
            nc.vector.scalar_tensor_tensor(
                out=red[:], in0=turns[:], scalar=-TURN_LO, in1=red1[:], op0=ALU.mult, op1=ALU.add
            )
            shifted = scratch.tile([P, width], F32, name="shifted")
            nc.gpsimd.tensor_scalar(
                out=shifted[:], in0=red[:], scalar1=0.5, scalar2=-math.pi / 4.0, op0=ALU.mult, op1=ALU.add
            )
            sc = scratch.tile([P, width], F32, name="sc")
            nc.scalar.activation(out=sc[:], in_=red[:], func=ACT.Sin, scale=0.5)
            ss = scratch.tile([P, width], F32, name="ss")
            nc.scalar.activation(out=ss[:], in_=shifted[:], func=ACT.Sin)
            qc = scratch.tile([P, width], F32, name="qc")
            nc.scalar.activation(out=qc[:], in_=sc[:], func=ACT.Square)
            qs = scratch.tile([P, width], F32, name="qs")
            nc.scalar.activation(out=qs[:], in_=ss[:], func=ACT.Square)
            cos_c = keep.tile([P, TABLE_TILES, HALF], F32, name="cos%d" % c)
            sin_c = keep.tile([P, TABLE_TILES, 2, HALF], F32, name="sin%d" % c)
            nc.gpsimd.tensor_scalar(
                out=cos_c[:], in0=qc[:].rearrange("p (j i) -> p j i", i=HALF),
                scalar1=-2.0, scalar2=1.0, op0=ALU.mult, op1=ALU.add,
            )
            nc.gpsimd.tensor_scalar(
                out=sin_c[:, :, 0, :], in0=qs[:].rearrange("p (j i) -> p j i", i=HALF),
                scalar1=-2.0, scalar2=1.0, op0=ALU.mult, op1=ALU.add,
            )
            nc.gpsimd.tensor_scalar(
                out=sin_c[:, :, 1, :], in0=qs[:].rearrange("p (j i) -> p j i", i=HALF),
                scalar1=2.0, scalar2=-1.0, op0=ALU.mult, op1=ALU.add,
            )
            cos_t.append(cos_c)
            sin_t.append(sin_c)

        def one_pass(acc, b, t, n0, n1, g):
            c, j = divmod(t, GROUP)
            nc.tensor.matmul_mx(
                out=acc[:],
                lhsT=code_pass(xc[c], g)[:, 2 * P * j : 2 * P * (j + 1)].bitcast(FP4X4),
                lhsT_scale=xs[c][:, g, P * j : P * (j + 1)],
                rhs=code_pass(wc[b], g)[:, 2 * n0 : 2 * n1].bitcast(FP4X4),
                rhs_scale=ws[b][:, g, n0:n1],
                start=(g == 0),
                stop=(g == PASSES - 1),
            )

        def project(b, t, n0, n1):
            acc = psum.tile([P, n1 - n0], F32, name="acc")
            for g in range(PASSES):
                one_pass(acc, b, t, n0, n1, g)
            return acc

        def products(acc, t, heads):
            c, j = divmod(t, TABLE_TILES)
            x_sb = acc
            by_cos = work.tile([P, heads, 2, HALF], F32, name="by_cos")
            by_sin = work.tile([P, heads, 2, HALF], F32, name="by_sin")
            nc.vector.tensor_tensor(
                out=by_cos[:].rearrange("p h a i -> p (h a) i"),
                in0=x_sb[:].rearrange("p (k i) -> p k i", i=HALF),
                in1=cos_t[c][:, j : j + 1, :].to_broadcast([P, 2 * heads, HALF]),
                op=ALU.mult,
            )
            nc.vector.tensor_tensor(
                out=by_sin[:].rearrange("p h a i -> p h (a i)"),
                in0=x_sb[:].rearrange("p (h k) -> p h k", k=HEAD),
                in1=sin_t[c][:, j : j + 1, :, :].rearrange("p j a i -> p j (a i)").to_broadcast([P, heads, HEAD]),
                op=ALU.mult,
            )
            return by_cos, by_sin

        def combine(by_cos, by_sin, b, t, n0, heads):
            y = work.tile([P, heads, 2, HALF], F32, name="y", bufs=4)
            nc.vector.tensor_tensor(out=y[:], in0=by_cos[:], in1=by_sin[:, :, ::-1, :], op=ALU.add)
            if b < Q_BLOCKS:
                dst, c0 = q_out, b * BLOCK + n0
            else:
                dst, c0 = k_out, (b - Q_BLOCKS) * BLOCK + n0
            nc.sync.dma_start(
                out=dst[t * P : (t + 1) * P, c0 : c0 + heads * HEAD],
                in_=y[:].rearrange("p h a i -> p (h a i)"),
            )

        units = []
        hooks = {}

        def at(index, what, arg):
            hooks.setdefault(max(index, 0), []).append((what, arg))

        blocks_in = 1
        tiles_in = GROUP
        for t in range(tiles_in):
            units.append((0, t))
        while blocks_in < BLOCKS or tiles_in < TOKEN_TILES:
            if blocks_in < BLOCKS:
                at(len(units) - LEAD, "block", blocks_in)
                for t in range(tiles_in):
                    units.append((blocks_in, t))
                blocks_in += 1
            if tiles_in < TOKEN_TILES:
                at(len(units) - LEAD, "chunk", tiles_in // GROUP)
                at(len(units) - 5, "tables", tiles_in // TABLE_TILES)
                for t in range(tiles_in, tiles_in + GROUP):
                    for b in range(blocks_in):
                        units.append((b, t))
                tiles_in += GROUP
        at(0, "tables", 0)

        pieces = []
        for index, (b, t) in enumerate(units):
            if index >= len(units) - 2:
                pieces.append((index, b, t, 0, HEAD))
                pieces.append((index, b, t, HEAD, BLOCK))
            else:
                pieces.append((index, b, t, 0, BLOCK))

        def run_hooks(index):
            for what, arg in hooks.get(index, []):
                if what == "block":
                    load_block(arg)
                elif what == "chunk":
                    load_chunk(arg)
                else:
                    build_tables(arg)

        first = []
        for index in range(GROUP):
            run_hooks(index)
            acc = psum.tile([P, BLOCK], F32, name="acc")
            first.append(acc)
        for g in range(PASSES):
            for t in range(GROUP):
                one_pass(first[t], 0, t, 0, BLOCK, g)

        pending = None
        for place, (index, b, t, n0, n1) in enumerate(pieces):
            heads = (n1 - n0) // HEAD
            if index < GROUP:
                acc = first[index]
            else:
                if n0 == 0:
                    run_hooks(index)
                acc = project(b, t, n0, n1)
            if place == len(pieces) - 1:
                combine(*pending)
                pending = None
            by_cos, by_sin = products(acc, t, heads)
            if pending is not None:
                combine(*pending)
            pending = (by_cos, by_sin, b, t, n0, heads)
        combine(*pending)
